import numpy as np
import ml_dtypes


def mxq(x, axis, fmt="e4m3"):
    dtype, down = {"e4m3": (ml_dtypes.float8_e4m3fn, 7), "e5m2": (ml_dtypes.float8_e5m2, 14)}[fmt]
    v = np.moveaxis(np.asarray(x, np.float32).astype(ml_dtypes.bfloat16).astype(np.float64), axis, -1)
    blocks = v.reshape(v.shape[:-1] + (-1, 32))
    amax = np.abs(blocks).max(-1, keepdims=True)
    byte = np.maximum(np.where(amax > 0, np.frexp(amax)[1] - 1 + 127, 0) - down, 1)
    scale = np.exp2(byte - 127.0)
    codes = (blocks / scale).astype(np.float32).astype(dtype).astype(np.float64)
    return np.moveaxis((codes * scale).reshape(v.shape), -1, axis)


WIDE = False


def mx_kscale(k):
    if not WIDE:
        return np.ones(k)
    levels = np.array([10, -10, 5, -5, 0])
    a = np.random.permutation(np.resize(levels, k // 512 * 4)).reshape(k // 512, 4)
    idx = np.arange(k)
    return np.exp2(a[idx // 512, idx % 128 // 32])


BF16 = ml_dtypes.bfloat16


def bf(x):
    return np.asarray(x, np.float32).astype(BF16)


def f64(x):
    return np.asarray(x).astype(np.float64)


E2M1 = np.array([0.0, 0.5, 1.0, 1.5, 2.0, 3.0, 4.0, 6.0, -0.0, -0.5, -1.0, -1.5, -2.0, -3.0, -4.0, -6.0])


def pack_weight(w, fmt):
    k, n = w.shape
    w = f64(bf(w)).reshape(k // 32, 32, n)
    amax = np.abs(w).max(1)
    if fmt == "e4m3":
        byte = np.frexp(amax)[1] - 1 + 127 - 7
    else:
        mant, ex = np.frexp(amax / 6.0)
        byte = np.where(mant > 0.5, ex, ex - 1) + 127
    byte = np.clip(np.where(amax > 0, byte, 1), 1, 254)
    scaled = (w * np.exp2(127.0 - byte)[:, None, :]).reshape(k, n).astype(np.float32)
    by_word = np.ascontiguousarray(scaled.reshape(k // 512, 128, 4, n).transpose(0, 1, 3, 2))
    if fmt == "e4m3":
        words = by_word.astype(ml_dtypes.float8_e4m3fn).view(np.uint8)
    else:
        c = by_word.astype(ml_dtypes.float4_e2m1fn).view(np.uint8) & 0xF
        words = c[..., 0::2] | (c[..., 1::2] << 4)
    return np.ascontiguousarray(words), np.ascontiguousarray(byte.astype(np.uint8).reshape(k // 512, 16, n))


def unpack_weight(words, scales, fmt):
    g, p, n, _ = words.shape
    if fmt == "e4m3":
        vals = np.ascontiguousarray(words).view(ml_dtypes.float8_e4m3fn).astype(np.float64)
    else:
        nib = np.empty((g, p, n, 4), np.uint8)
        nib[..., 0::2] = words & 0xF
        nib[..., 1::2] = words >> 4
        vals = E2M1[nib]
    vals = vals * np.repeat(np.exp2(scales.astype(np.float64) - 127.0), 8, axis=1)[..., None]
    return vals.transpose(0, 1, 3, 2).reshape(g * 512, n)


B, M, D, E = 2, 512, 1024, 1024
HALF = E // 2
FMT = "e4m3"


def rope_cos_sin():
    i = np.arange(HALF, dtype=np.float64)
    theta = np.power(10000.0, -2.0 * (i - 1.0) / E)
    pos = np.arange(M, dtype=np.float64)
    ang = pos[:, None] * theta[None, :]
    return np.cos(ang), np.sin(ang)


def rotate(t, cos, sin):
    te = t[..., 0::2]
    to = t[..., 1::2]
    re = te * cos + to * sin
    ro = -te * sin + to * cos
    return np.stack((re, ro), axis=-1).reshape(t.shape)


def setup_inputs():
    s = mx_kscale(D)
    sc = 1.0 / np.sqrt(D)
    x = bf(np.random.standard_normal((B, M, D)) * s)
    w_q = np.random.standard_normal((E, D)) * sc / s[None, :]
    w_k = np.random.standard_normal((E, D)) * sc / s[None, :]
    w_q_words, w_q_scales = pack_weight(w_q.T, FMT)
    w_k_words, w_k_scales = pack_weight(w_k.T, FMT)
    return {"x": x,
            "w_q_words": w_q_words, "w_q_scales": w_q_scales,
            "w_k_words": w_k_words, "w_k_scales": w_k_scales}


def reference(x, w_q_words, w_q_scales, w_k_words, w_k_scales):
    xq = mxq(f64(x), 2, "e4m3")
    q = xq @ unpack_weight(w_q_words, w_q_scales, FMT)
    k = xq @ unpack_weight(w_k_words, w_k_scales, FMT)
    cos, sin = rope_cos_sin()
    return rotate(q, cos, sin), rotate(k, cos, sin)

@@ -1,0 +1,228 @@
+import math
+from contextlib import ExitStack
+
+import concourse.mybir as mybir
+from concourse.masks import make_identity
+
+F32 = mybir.dt.float32
+BF16 = mybir.dt.bfloat16
+I32 = mybir.dt.int32
+U32 = mybir.dt.uint32
+U8 = mybir.dt.uint8
+FP8X4 = mybir.dt.float8_e4m3fn_x4
+ALU = mybir.AluOpType
+ACT = mybir.ActivationFunctionType
+
+P = 128
+BATCH = 2
+POSITIONS = 512
+D_IN = 1024
+D_OUT = 1024
+PAIRS = D_OUT // 2
+POS_TILES = POSITIONS // P
+K_PASS = 4 * P
+PASSES = D_IN // K_PASS
+N_TILE = 512
+CHUNKS = D_OUT // N_TILE
+CHUNK_PAIRS = N_TILE // 2
+WORDS_PER_PASS = K_PASS // 2
+
+FINE = 16
+COARSE = PAIRS // FINE
+
+RATIO = 10000.0 ** (-2.0 / D_OUT)
+
+FLOPS = 2 * BATCH * POSITIONS * D_IN * 2 * D_OUT
+
+
+def tile_ropemaskedattentionhead_pa_kernel(
+    tc, x, w_q_words, w_q_scales, w_k_words, w_k_scales, out_0, out_1
+):
+    nc = tc.nc
+    weights = ((w_q_words, w_q_scales, out_0), (w_k_words, w_k_scales, out_1))
+
+    with ExitStack() as ctx:
+        keep = ctx.enter_context(tc.tile_pool(name="keep", bufs=1))
+        stage = ctx.enter_context(tc.tile_pool(name="stage", bufs=2))
+        products = ctx.enter_context(tc.tile_pool(name="products", bufs=3))
+        results = ctx.enter_context(tc.tile_pool(name="results", bufs=4))
+        psum_x = ctx.enter_context(tc.psum_pool(name="psum_x", bufs=2))
+        psum_acc = ctx.enter_context(tc.psum_pool(name="psum_acc", bufs=6))
+
+        x_sb = keep.tile([P, BATCH, POS_TILES, D_IN], BF16)
+        x_codes = keep.tile([P, BATCH, POS_TILES, PASSES * P], U32, align_bytes=64)
+        x_scales = keep.tile([P, BATCH, POS_TILES, PASSES * P], U8, align_bytes=64)
+        w_codes = keep.tile([P, 2, PASSES, D_OUT], U32, align_bytes=64)
+        w_planes = keep.tile([P, D_OUT], U8, align_bytes=64)
+        identity = keep.tile([P, P], F32)
+        theta = keep.tile([P, PAIRS], F32)
+        fine = keep.tile([P, FINE], F32)
+        coarse = keep.tile([P, COARSE], F32)
+        position = keep.tile([P, POS_TILES], I32)
+        turns = keep.tile([P, POS_TILES], F32)
+        table = keep.tile([P, POS_TILES, 2, PAIRS, 2], F32)
+
+        def load_x(b, t):
+            nc.sync.dma_start(out=x_sb[:, b, t, :], in_=x[b, t * P : (t + 1) * P, :])
+
+        def load_weight_scales(w):
+            scales = weights[w][1]
+            for quadrant in range(4):
+                first = 32 * quadrant + 4 * PASSES * w
+                nc.sync.dma_start(
+                    out=w_planes[first : first + 4 * PASSES, :].bitcast(I32),
+                    in_=scales[:, 4 * quadrant : 4 * quadrant + 4, :].bitcast(I32),
+                )
+
+        def load_weight_codes(w, c):
+            columns = slice(c * N_TILE, (c + 1) * N_TILE)
+            for g in range(PASSES):
+                words = weights[w][0][g].rearrange("p n v -> p (n v)").bitcast(I32)
+                nc.sync.dma_start(out=w_codes[:, w, g, columns].bitcast(I32), in_=words[:, columns])
+
+        nc.vector.memset(w_planes[:].bitcast(I32), 0)
+        for b in range(BATCH):
+            load_x(b, 0)
+        for w in range(2):
+            load_weight_scales(w)
+            load_weight_codes(w, 0)
+        for w in range(2):
+            load_weight_codes(w, 1)
+        for t in range(1, POS_TILES):
+            for b in range(BATCH):
+                load_x(b, t)
+
+        nc.gpsimd.iota(position[:], pattern=[[P, POS_TILES]], base=0, channel_multiplier=1)
+        make_identity(nc, identity[:])
+        nc.vector.tensor_scalar_mul(
+            out=turns[:], in0=position[:], scalar1=1.0 / (2.0 * math.pi * RATIO)
+        )
+
+        def powers(out, ratio, count):
+            nc.vector.memset(out[:, 0:1], 1.0)
+            n = 1
+            while n < count:
+                nc.vector.tensor_scalar_mul(
+                    out=out[:, n : 2 * n], in0=out[:, 0:n], scalar1=ratio**n
+                )
+                n = 2 * n
+
+        powers(fine, RATIO, FINE)
+        powers(coarse, RATIO**FINE, COARSE)
+        for c in range(CHUNKS):
+            rows = CHUNK_PAIRS // FINE
+            nc.vector.tensor_tensor(
+                out=theta[:, c * CHUNK_PAIRS : (c + 1) * CHUNK_PAIRS].rearrange(
+                    "p (a b) -> p a b", b=FINE
+                ),
+                in0=coarse[:, c * rows : (c + 1) * rows].unsqueeze(2).to_broadcast([P, rows, FINE]),
+                in1=fine[:].unsqueeze(1).to_broadcast([P, rows, FINE]),
+                op=ALU.mult,
+            )
+
+        def build_table(t, c):
+            pairs = slice(c * CHUNK_PAIRS, (c + 1) * CHUNK_PAIRS)
+            scale = turns[:, t : t + 1]
+            whole = stage.tile([P, CHUNK_PAIRS], U32)
+            nc.scalar.activation(out=whole[:], in_=theta[:, pairs], func=ACT.Copy, scale=scale)
+            phase = stage.tile([P, 3, CHUNK_PAIRS], F32)
+            nc.vector.scalar_tensor_tensor(
+                out=phase[:, 0, :],
+                in0=theta[:, pairs],
+                scalar=scale,
+                in1=whole[:].bitcast(I32),
+                op0=ALU.mult,
+                op1=ALU.subtract,
+            )
+            nc.scalar.activation(out=phase[:, 1, :], in_=phase[:, 0, :], func=ACT.Abs)
+            nc.scalar.activation(
+                out=phase[:, 1, :], in_=phase[:, 1, :], func=ACT.Copy, scale=-1.0, bias=0.25
+            )
+            nc.scalar.mul(out=phase[:, 2, :], in_=phase[:, 0, :], mul=-1.0)
+            for half in range(2):
+                first = 1 - half
+                nc.scalar.activation(
+                    out=table[:, t, half, pairs, :],
+                    in_=phase[:, first : first + 2, :].rearrange("p w i -> p i w"),
+                    func=ACT.Sin,
+                    scale=2.0 * math.pi,
+                )
+
+        def quantise_x(b, t):
+            x_words = x_sb[:, b, t, :].bitcast(F32)
+            flipped = psum_x.tile([P, PASSES, 2, P], F32)
+            for g in range(PASSES):
+                for u in range(2):
+                    nc.tensor.transpose(
+                        flipped[:, g, u, :],
+                        x_words[:, WORDS_PER_PASS * g + u : WORDS_PER_PASS * (g + 1) : 2],
+                        identity[:],
+                    )
+            grouped = stage.tile([P, PASSES, P, 4], BF16, align_bytes=64)
+            if t == 0:
+                nc.vector.tensor_copy(
+                    out=grouped[:].bitcast(F32), in_=flipped[:].rearrange("p g u r -> p g r u")
+                )
+            else:
+                nc.scalar.copy(
+                    out=grouped[:].bitcast(F32), in_=flipped[:].rearrange("p g u r -> p g r u")
+                )
+            nc.vector.quantize_mx(
+                out=x_codes[:, b, t, :].bitcast(FP8X4),
+                scales=x_scales[:, b, t, :],
+                in_=grouped[:].rearrange("p g r v -> p (g r v)"),
+            )
+
+        def project_and_rotate(t, c, w):
+            columns = slice(c * N_TILE, (c + 1) * N_TILE)
+            pairs = slice(c * CHUNK_PAIRS, (c + 1) * CHUNK_PAIRS)
+            product = products.tile([P, 2, BATCH, CHUNK_PAIRS, 2], F32)
+            for b in range(BATCH):
+                acc = psum_acc.tile([P, N_TILE], F32)
+                for g in range(PASSES):
+                    plane_start = 4 * (PASSES * w + g)
+                    nc.tensor.matmul_mx(
+                        out=acc[:],
+                        lhsT=x_codes[:, b, t, g * P : (g + 1) * P].bitcast(FP8X4),
+                        lhsT_scale=x_scales[:, b, t, g * P : (g + 1) * P],
+                        rhs=w_codes[:, w, g, columns].bitcast(FP8X4),
+                        rhs_scale=w_planes[plane_start:P, columns],
+                        start=(g == 0),
+                        stop=(g == PASSES - 1),
+                    )
+                nc.vector.tensor_tensor(
+                    out=product[:, :, b, :, :],
+                    in0=acc[:]
+                    .rearrange("p (i h) -> p h i", h=2)
+                    .unsqueeze(3)
+                    .to_broadcast([P, 2, CHUNK_PAIRS, 2]),
+                    in1=table[:, t, :, pairs, :],
+                    op=ALU.mult,
+                )
+            rotated = results.tile([P, BATCH, N_TILE], F32)
+            last = (t, c, w) == (POS_TILES - 1, CHUNKS - 1, 1)
+            adder = nc.vector if last else nc.gpsimd
+            adder.tensor_tensor(
+                out=rotated[:].rearrange("p b n -> p (b n)"),
+                in0=product[:, 0].rearrange("p b i w -> p (b i w)"),
+                in1=product[:, 1].rearrange("p b i w -> p (b i w)"),
+                op=ALU.add,
+            )
+            nc.sync.dma_start(
+                out=weights[w][2][:, t * P : (t + 1) * P, columns].rearrange("b p n -> p b n"),
+                in_=rotated[:],
+            )
+
+        def prepare(t, c):
+            build_table(t, c)
+            if c == 0:
+                for b in range(BATCH):
+                    quantise_x(b, t)
+
+        groups = [(t, c) for t in range(POS_TILES) for c in range(CHUNKS)]
+        prepare(0, 0)
+        for n, (t, c) in enumerate(groups):
+            if n + 1 < len(groups):
+                prepare(groups[n + 1][0], groups[n + 1][1])
+            for w in range(2):
+                project_and_rotate(t, c, w)

@@ -26,7 +26,6 @@ N_TILE = 512
 CHUNKS = D_OUT // N_TILE
 CHUNK_PAIRS = N_TILE // 2
 WORDS_PER_PASS = K_PASS // 2
-
 FINE = 16
 COARSE = PAIRS // FINE
 
@@ -48,6 +47,7 @@ def tile_ropemaskedattentionhead_pa_kernel(
         results = ctx.enter_context(tc.tile_pool(name="results", bufs=4))
         psum_x = ctx.enter_context(tc.psum_pool(name="psum_x", bufs=2))
         psum_acc = ctx.enter_context(tc.psum_pool(name="psum_acc", bufs=6))
+        ctx.enter_context(tc.manual_schedule())
 
         x_sb = keep.tile([P, BATCH, POS_TILES, D_IN], BF16)
         x_codes = keep.tile([P, BATCH, POS_TILES, PASSES * P], U32, align_bytes=64)
@@ -55,9 +55,9 @@ def tile_ropemaskedattentionhead_pa_kernel(
         w_codes = keep.tile([P, 2, PASSES, D_OUT], U32, align_bytes=64)
         w_planes = keep.tile([P, D_OUT], U8, align_bytes=64)
         identity = keep.tile([P, P], F32)
-        theta = keep.tile([P, PAIRS], F32)
         fine = keep.tile([P, FINE], F32)
         coarse = keep.tile([P, COARSE], F32)
+        theta = keep.tile([P, PAIRS], F32)
         position = keep.tile([P, POS_TILES], I32)
         turns = keep.tile([P, POS_TILES], F32)
         table = keep.tile([P, POS_TILES, 2, PAIRS, 2], F32)
@@ -86,30 +86,34 @@ def tile_ropemaskedattentionhead_pa_kernel(
         for w in range(2):
             load_weight_scales(w)
             load_weight_codes(w, 0)
+        for b in range(BATCH):
+            load_x(b, 1)
         for w in range(2):
             load_weight_codes(w, 1)
-        for t in range(1, POS_TILES):
+        for t in range(2, POS_TILES):
             for b in range(BATCH):
                 load_x(b, t)
 
         nc.gpsimd.iota(position[:], pattern=[[P, POS_TILES]], base=0, channel_multiplier=1)
         make_identity(nc, identity[:])
+
+        nc.vector.memset(fine[:, 0:1], 1.0)
+        nc.vector.memset(coarse[:, 0:1], 1.0)
+        n = 1
+        while n < COARSE:
+            if n < FINE:
+                nc.vector.tensor_scalar_mul(
+                    out=fine[:, n : 2 * n], in0=fine[:, 0:n], scalar1=RATIO**n
+                )
+            nc.vector.tensor_scalar_mul(
+                out=coarse[:, n : 2 * n], in0=coarse[:, 0:n], scalar1=RATIO ** (FINE * n)
+            )
+            n = 2 * n
         nc.vector.tensor_scalar_mul(
             out=turns[:], in0=position[:], scalar1=1.0 / (2.0 * math.pi * RATIO)
         )
 
-        def powers(out, ratio, count):
-            nc.vector.memset(out[:, 0:1], 1.0)
-            n = 1
-            while n < count:
-                nc.vector.tensor_scalar_mul(
-                    out=out[:, n : 2 * n], in0=out[:, 0:n], scalar1=ratio**n
-                )
-                n = 2 * n
-
-        powers(fine, RATIO, FINE)
-        powers(coarse, RATIO**FINE, COARSE)
-        for c in range(CHUNKS):
+        def build_theta(c):
             rows = CHUNK_PAIRS // FINE
             nc.vector.tensor_tensor(
                 out=theta[:, c * CHUNK_PAIRS : (c + 1) * CHUNK_PAIRS].rearrange(
@@ -120,17 +124,24 @@ def tile_ropemaskedattentionhead_pa_kernel(
                 op=ALU.mult,
             )
 
-        def build_table(t, c):
-            pairs = slice(c * CHUNK_PAIRS, (c + 1) * CHUNK_PAIRS)
-            scale = turns[:, t : t + 1]
-            whole = stage.tile([P, CHUNK_PAIRS], U32)
-            nc.scalar.activation(out=whole[:], in_=theta[:, pairs], func=ACT.Copy, scale=scale)
-            phase = stage.tile([P, 3, CHUNK_PAIRS], F32)
+        whole_turns = {}
+
+        def start_table(t, first_pair, count):
+            pairs = slice(first_pair, first_pair + count)
+            whole = stage.tile([P, count], U32, name="whole")
+            nc.scalar.activation(
+                out=whole[:], in_=theta[:, pairs], func=ACT.Copy, scale=turns[:, t : t + 1]
+            )
+            whole_turns[(t, first_pair)] = whole
+
+        def finish_table(t, first_pair, count):
+            pairs = slice(first_pair, first_pair + count)
+            phase = stage.tile([P, 3, count], F32)
             nc.vector.scalar_tensor_tensor(
                 out=phase[:, 0, :],
                 in0=theta[:, pairs],
-                scalar=scale,
-                in1=whole[:].bitcast(I32),
+                scalar=turns[:, t : t + 1],
+                in1=whole_turns[(t, first_pair)][:].bitcast(I32),
                 op0=ALU.mult,
                 op1=ALU.subtract,
             )
@@ -148,7 +159,9 @@ def tile_ropemaskedattentionhead_pa_kernel(
                     scale=2.0 * math.pi,
                 )
 
-        def quantise_x(b, t):
+        grouped_x = {}
+
+        def flip_x(b, t):
             x_words = x_sb[:, b, t, :].bitcast(F32)
             flipped = psum_x.tile([P, PASSES, 2, P], F32)
             for g in range(PASSES):
@@ -158,7 +171,7 @@ def tile_ropemaskedattentionhead_pa_kernel(
                         x_words[:, WORDS_PER_PASS * g + u : WORDS_PER_PASS * (g + 1) : 2],
                         identity[:],
                     )
-            grouped = stage.tile([P, PASSES, P, 4], BF16, align_bytes=64)
+            grouped = stage.tile([P, PASSES, P, 4], BF16, align_bytes=64, name="grouped")
             if t == 0:
                 nc.vector.tensor_copy(
                     out=grouped[:].bitcast(F32), in_=flipped[:].rearrange("p g u r -> p g r u")
@@ -167,10 +180,13 @@ def tile_ropemaskedattentionhead_pa_kernel(
                 nc.scalar.copy(
                     out=grouped[:].bitcast(F32), in_=flipped[:].rearrange("p g u r -> p g r u")
                 )
+            grouped_x[(b, t)] = grouped
+
+        def quantise_x(b, t):
             nc.vector.quantize_mx(
                 out=x_codes[:, b, t, :].bitcast(FP8X4),
                 scales=x_scales[:, b, t, :],
-                in_=grouped[:].rearrange("p g r v -> p (g r v)"),
+                in_=grouped_x[(b, t)][:].rearrange("p g r v -> p (g r v)"),
             )
 
         def project_and_rotate(t, c, w):
@@ -213,16 +229,28 @@ def tile_ropemaskedattentionhead_pa_kernel(
                 in_=rotated[:],
             )
 
-        def prepare(t, c):
-            build_table(t, c)
-            if c == 0:
-                for b in range(BATCH):
-                    quantise_x(b, t)
+        for c in range(CHUNKS):
+            build_theta(c)
+            start_table(0, c * CHUNK_PAIRS, CHUNK_PAIRS)
+        for c in range(CHUNKS):
+            finish_table(0, c * CHUNK_PAIRS, CHUNK_PAIRS)
+        start_table(1, 0, PAIRS)
+        for b in range(BATCH):
+            flip_x(b, 0)
+            quantise_x(b, 0)
 
-        groups = [(t, c) for t in range(POS_TILES) for c in range(CHUNKS)]
-        prepare(0, 0)
-        for n, (t, c) in enumerate(groups):
-            if n + 1 < len(groups):
-                prepare(groups[n + 1][0], groups[n + 1][1])
-            for w in range(2):
-                project_and_rotate(t, c, w)
+        for t in range(POS_TILES):
+            more = t + 1 < POS_TILES
+            project_and_rotate(t, 0, 0)
+            if more:
+                for b in range(BATCH):
+                    flip_x(b, t + 1)
+            project_and_rotate(t, 0, 1)
+            if more:
+                finish_table(t + 1, 0, PAIRS)
+                for b in range(BATCH):
+                    quantise_x(b, t + 1)
+            if t + 2 < POS_TILES:
+                start_table(t + 2, 0, PAIRS)
+            project_and_rotate(t, 1, 0)
+            project_and_rotate(t, 1, 1)

@@ -57,6 +57,7 @@ def tile_ropemaskedattentionhead_pa_kernel(
         identity = keep.tile([P, P], F32)
         fine = keep.tile([P, FINE], F32)
         coarse = keep.tile([P, COARSE], F32)
+        table_warmer = keep.tile([P, 1], F32)
         theta = keep.tile([P, PAIRS], F32)
         position = keep.tile([P, POS_TILES], I32)
         turns = keep.tile([P, POS_TILES], F32)
@@ -80,6 +81,9 @@ def tile_ropemaskedattentionhead_pa_kernel(
                 words = weights[w][0][g].rearrange("p n v -> p (n v)").bitcast(I32)
                 nc.sync.dma_start(out=w_codes[:, w, g, columns].bitcast(I32), in_=words[:, columns])
 
+        nc.vector.memset(fine[:, 0:1], 1.0)
+        nc.scalar.activation(out=table_warmer[:], in_=fine[:, 0:1], func=ACT.Sin)
+
         nc.vector.memset(w_planes[:].bitcast(I32), 0)
         for b in range(BATCH):
             load_x(b, 0)
@@ -97,7 +101,6 @@ def tile_ropemaskedattentionhead_pa_kernel(
         nc.gpsimd.iota(position[:], pattern=[[P, POS_TILES]], base=0, channel_multiplier=1)
         make_identity(nc, identity[:])
 
-        nc.vector.memset(fine[:, 0:1], 1.0)
         nc.vector.memset(coarse[:, 0:1], 1.0)
         n = 1
         while n < COARSE:
@@ -189,6 +192,22 @@ def tile_ropemaskedattentionhead_pa_kernel(
                 in_=grouped_x[(b, t)][:].rearrange("p g r v -> p (g r v)"),
             )
 
+        def add_and_store(adder, product, t, c, w, first_batch, batches):
+            chosen = slice(first_batch, first_batch + batches)
+            rotated = results.tile([P, batches, N_TILE], F32)
+            adder.tensor_tensor(
+                out=rotated[:].rearrange("p b n -> p (b n)"),
+                in0=product[:, 0, chosen].rearrange("p b i w -> p (b i w)"),
+                in1=product[:, 1, chosen].rearrange("p b i w -> p (b i w)"),
+                op=ALU.add,
+            )
+            nc.sync.dma_start(
+                out=weights[w][2][
+                    chosen, t * P : (t + 1) * P, c * N_TILE : (c + 1) * N_TILE
+                ].rearrange("b p n -> p b n"),
+                in_=rotated[:],
+            )
+
         def project_and_rotate(t, c, w):
             columns = slice(c * N_TILE, (c + 1) * N_TILE)
             pairs = slice(c * CHUNK_PAIRS, (c + 1) * CHUNK_PAIRS)
@@ -215,19 +234,11 @@ def tile_ropemaskedattentionhead_pa_kernel(
                     in1=table[:, t, :, pairs, :],
                     op=ALU.mult,
                 )
-            rotated = results.tile([P, BATCH, N_TILE], F32)
-            last = (t, c, w) == (POS_TILES - 1, CHUNKS - 1, 1)
-            adder = nc.vector if last else nc.gpsimd
-            adder.tensor_tensor(
-                out=rotated[:].rearrange("p b n -> p (b n)"),
-                in0=product[:, 0].rearrange("p b i w -> p (b i w)"),
-                in1=product[:, 1].rearrange("p b i w -> p (b i w)"),
-                op=ALU.add,
-            )
-            nc.sync.dma_start(
-                out=weights[w][2][:, t * P : (t + 1) * P, columns].rearrange("b p n -> p b n"),
-                in_=rotated[:],
-            )
+            if (t, c, w) == (POS_TILES - 1, CHUNKS - 1, 1):
+                for b in range(BATCH):
+                    add_and_store(nc.vector, product, t, c, w, b, 1)
+            else:
+                add_and_store(nc.gpsimd, product, t, c, w, 0, BATCH)
 
         for c in range(CHUNKS):
             build_theta(c)

@@ -29,6 +29,8 @@ WORDS_PER_PASS = K_PASS // 2
 FINE = 16
 COARSE = PAIRS // FINE
 
+FINE_STEP = 32
+
 RATIO = 10000.0 ** (-2.0 / D_OUT)
 
 FLOPS = 2 * BATCH * POSITIONS * D_IN * 2 * D_OUT
@@ -50,8 +52,8 @@ def tile_ropemaskedattentionhead_pa_kernel(
         ctx.enter_context(tc.manual_schedule())
 
         x_sb = keep.tile([P, BATCH, POS_TILES, D_IN], BF16)
-        x_codes = keep.tile([P, BATCH, POS_TILES, PASSES * P], U32, align_bytes=64)
-        x_scales = keep.tile([P, BATCH, POS_TILES, PASSES * P], U8, align_bytes=64)
+        x_codes = keep.tile([P, POS_TILES, BATCH, PASSES * P], U32, align_bytes=64)
+        x_scales = keep.tile([P, POS_TILES, BATCH, PASSES * P], U8, align_bytes=64)
         w_codes = keep.tile([P, 2, PASSES, D_OUT], U32, align_bytes=64)
         w_planes = keep.tile([P, D_OUT], U8, align_bytes=64)
         identity = keep.tile([P, P], F32)
@@ -62,6 +64,8 @@ def tile_ropemaskedattentionhead_pa_kernel(
         position = keep.tile([P, POS_TILES], I32)
         turns = keep.tile([P, POS_TILES], F32)
         table = keep.tile([P, POS_TILES, 2, PAIRS, 2], F32)
+        all_phases = keep.tile([P, POS_TILES, 3, PAIRS], F32)
+        early_whole = keep.tile([P, POS_TILES, PAIRS], I32)
 
         def load_x(b, t):
             nc.sync.dma_start(out=x_sb[:, b, t, :], in_=x[b, t * P : (t + 1) * P, :])
@@ -127,27 +131,64 @@ def tile_ropemaskedattentionhead_pa_kernel(
                 op=ALU.mult,
             )
 
-        whole_turns = {}
+        def reduced_pairs(t, step):
+            last_position = P * (t + 1) - 1
+            n = 0
+            while n < PAIRS and last_position * RATIO ** (n - 1) > 0.49 * 2.0 * math.pi:
+                n += step
+            return n
 
-        def start_table(t, first_pair, count):
-            pairs = slice(first_pair, first_pair + count)
-            whole = stage.tile([P, count], U32, name="whole")
-            nc.scalar.activation(
-                out=whole[:], in_=theta[:, pairs], func=ACT.Copy, scale=turns[:, t : t + 1]
+        whole_turns = {}
+        phases = {}
+
+        def start_table(t, first_pair, count, step):
+            n = min(max(reduced_pairs(t, step) - first_pair, 0), count)
+            phase = all_phases[:, t, :, first_pair : first_pair + count]
+            phases[(t, first_pair)] = (phase, n)
+            if n > 0 and t == 0:
+                whole = stage.tile([P, n], U32, name="whole")
+                nc.scalar.activation(
+                    out=whole[:],
+                    in_=theta[:, first_pair : first_pair + n],
+                    func=ACT.Copy,
+                    scale=turns[:, t : t + 1],
+                )
+                whole_turns[(t, first_pair)] = whole[:].bitcast(I32)
+            if n < count:
+                nc.scalar.activation(
+                    out=phase[:, 0, n:count],
+                    in_=theta[:, first_pair + n : first_pair + count],
+                    func=ACT.Copy,
+                    scale=turns[:, t : t + 1],
+                )
+
+        def whole_turns_early(t):
+            n = reduced_pairs(t, FINE_STEP)
+            nc.gpsimd.tensor_scalar(
+                out=early_whole[:, t, 0:n],
+                in0=theta[:, 0:n],
+                scalar1=turns[:, t : t + 1],
+                scalar2=0.0,
+                op0=ALU.mult,
+                op1=ALU.add,
             )
-            whole_turns[(t, first_pair)] = whole
+            whole_turns[(t, 0)] = early_whole[:, t, 0:n]
+
+        def reduce_angle(t, first_pair):
+            phase, n = phases[(t, first_pair)]
+            if n > 0:
+                nc.vector.scalar_tensor_tensor(
+                    out=phase[:, 0, 0:n],
+                    in0=theta[:, first_pair : first_pair + n],
+                    scalar=turns[:, t : t + 1],
+                    in1=whole_turns[(t, first_pair)],
+                    op0=ALU.mult,
+                    op1=ALU.subtract,
+                )
 
         def finish_table(t, first_pair, count):
             pairs = slice(first_pair, first_pair + count)
-            phase = stage.tile([P, 3, count], F32)
-            nc.vector.scalar_tensor_tensor(
-                out=phase[:, 0, :],
-                in0=theta[:, pairs],
-                scalar=turns[:, t : t + 1],
-                in1=whole_turns[(t, first_pair)][:].bitcast(I32),
-                op0=ALU.mult,
-                op1=ALU.subtract,
-            )
+            phase, n = phases[(t, first_pair)]
             nc.scalar.activation(out=phase[:, 1, :], in_=phase[:, 0, :], func=ACT.Abs)
             nc.scalar.activation(
                 out=phase[:, 1, :], in_=phase[:, 1, :], func=ACT.Copy, scale=-1.0, bias=0.25
@@ -174,22 +215,22 @@ def tile_ropemaskedattentionhead_pa_kernel(
                         x_words[:, WORDS_PER_PASS * g + u : WORDS_PER_PASS * (g + 1) : 2],
                         identity[:],
                     )
-            grouped = stage.tile([P, PASSES, P, 4], BF16, align_bytes=64, name="grouped")
-            if t == 0:
-                nc.vector.tensor_copy(
-                    out=grouped[:].bitcast(F32), in_=flipped[:].rearrange("p g u r -> p g r u")
-                )
-            else:
-                nc.scalar.copy(
-                    out=grouped[:].bitcast(F32), in_=flipped[:].rearrange("p g u r -> p g r u")
-                )
-            grouped_x[(b, t)] = grouped
+            if b == 0:
+                both_batches = stage.tile([P, BATCH, PASSES, P, 4], BF16, align_bytes=64, name="grouped")
+                grouped_x[t] = both_batches
+            grouped = grouped_x[t][:, b].rearrange("p g r v -> p g (r v)").bitcast(F32)
+            copier = nc.vector.tensor_copy if t == 0 else nc.scalar.copy
+            copier(
+                out=grouped.rearrange("p g (r u) -> p g r u", u=2),
+                in_=flipped[:].rearrange("p g u r -> p g r u"),
+            )
 
-        def quantise_x(b, t):
+        def quantise_x(t, first_batch, batches):
+            chosen = slice(first_batch, first_batch + batches)
             nc.vector.quantize_mx(
-                out=x_codes[:, b, t, :].bitcast(FP8X4),
-                scales=x_scales[:, b, t, :],
-                in_=grouped_x[(b, t)][:].rearrange("p g r v -> p (g r v)"),
+                out=x_codes[:, t, chosen, :].rearrange("p b n -> p (b n)").bitcast(FP8X4),
+                scales=x_scales[:, t, chosen, :].rearrange("p b n -> p (b n)"),
+                in_=grouped_x[t][:, chosen].rearrange("p b g r v -> p (b g r v)"),
             )
 
         def add_and_store(adder, product, t, c, w, first_batch, batches):
@@ -218,8 +259,8 @@ def tile_ropemaskedattentionhead_pa_kernel(
                     plane_start = 4 * (PASSES * w + g)
                     nc.tensor.matmul_mx(
                         out=acc[:],
-                        lhsT=x_codes[:, b, t, g * P : (g + 1) * P].bitcast(FP8X4),
-                        lhsT_scale=x_scales[:, b, t, g * P : (g + 1) * P],
+                        lhsT=x_codes[:, t, b, g * P : (g + 1) * P].bitcast(FP8X4),
+                        lhsT_scale=x_scales[:, t, b, g * P : (g + 1) * P],
                         rhs=w_codes[:, w, g, columns].bitcast(FP8X4),
                         rhs_scale=w_planes[plane_start:P, columns],
                         start=(g == 0),
@@ -242,13 +283,19 @@ def tile_ropemaskedattentionhead_pa_kernel(
 
         for c in range(CHUNKS):
             build_theta(c)
-            start_table(0, c * CHUNK_PAIRS, CHUNK_PAIRS)
+            start_table(0, c * CHUNK_PAIRS, CHUNK_PAIRS, CHUNK_PAIRS)
+        for t in range(1, POS_TILES):
+            whole_turns_early(t)
         for c in range(CHUNKS):
+            reduce_angle(0, c * CHUNK_PAIRS)
             finish_table(0, c * CHUNK_PAIRS, CHUNK_PAIRS)
-        start_table(1, 0, PAIRS)
+        for t in range(1, POS_TILES):
+            start_table(t, 0, PAIRS, FINE_STEP)
+        for t in range(1, POS_TILES - 1):
+            reduce_angle(t, 0)
         for b in range(BATCH):
             flip_x(b, 0)
-            quantise_x(b, 0)
+            quantise_x(0, b, 1)
 
         for t in range(POS_TILES):
             more = t + 1 < POS_TILES
@@ -258,10 +305,9 @@ def tile_ropemaskedattentionhead_pa_kernel(
                     flip_x(b, t + 1)
             project_and_rotate(t, 0, 1)
             if more:
+                if t == 0:
+                    reduce_angle(POS_TILES - 1, 0)
                 finish_table(t + 1, 0, PAIRS)
-                for b in range(BATCH):
-                    quantise_x(b, t + 1)
-            if t + 2 < POS_TILES:
-                start_table(t + 2, 0, PAIRS)
+                quantise_x(t + 1, 0, BATCH)
             project_and_rotate(t, 1, 0)
             project_and_rotate(t, 1, 1)

@@ -45,8 +45,8 @@ def tile_ropemaskedattentionhead_pa_kernel(
     with ExitStack() as ctx:
         keep = ctx.enter_context(tc.tile_pool(name="keep", bufs=1))
         stage = ctx.enter_context(tc.tile_pool(name="stage", bufs=2))
-        products = ctx.enter_context(tc.tile_pool(name="products", bufs=3))
-        results = ctx.enter_context(tc.tile_pool(name="results", bufs=4))
+        products = ctx.enter_context(tc.tile_pool(name="products", bufs=4))
+        results = ctx.enter_context(tc.tile_pool(name="results", bufs=8))
         psum_x = ctx.enter_context(tc.psum_pool(name="psum_x", bufs=2))
         psum_acc = ctx.enter_context(tc.psum_pool(name="psum_acc", bufs=6))
         ctx.enter_context(tc.manual_schedule())
@@ -237,9 +237,9 @@ def tile_ropemaskedattentionhead_pa_kernel(
             chosen = slice(first_batch, first_batch + batches)
             rotated = results.tile([P, batches, N_TILE], F32)
             adder.tensor_tensor(
-                out=rotated[:].rearrange("p b n -> p (b n)"),
-                in0=product[:, 0, chosen].rearrange("p b i w -> p (b i w)"),
-                in1=product[:, 1, chosen].rearrange("p b i w -> p (b i w)"),
+                out=rotated[:],
+                in0=product[:, chosen, 0].rearrange("p b i w -> p b (i w)"),
+                in1=product[:, chosen, 1].rearrange("p b i w -> p b (i w)"),
                 op=ALU.add,
             )
             nc.sync.dma_start(
@@ -249,12 +249,38 @@ def tile_ropemaskedattentionhead_pa_kernel(
                 in_=rotated[:],
             )
 
+        late_adds = []
+        waiting = []
+
+        def add_on_tensor_engine():
+            for product, t, c, w, b in waiting:
+                total = psum_acc.tile([P, N_TILE], F32, name="acc")
+                for h in range(2):
+                    nc.tensor.matmul(
+                        out=total[:],
+                        lhsT=identity[:],
+                        rhs=product[:, b, h].rearrange("p i v -> p (i v)"),
+                        start=(h == 0),
+                        stop=(h == 1),
+                    )
+                rotated = results.tile([P, 1, N_TILE], F32, name="rotated")
+                nc.scalar.copy(out=rotated[:, 0, :], in_=total[:])
+                nc.sync.dma_start(
+                    out=weights[w][2][
+                        b : b + 1, t * P : (t + 1) * P, c * N_TILE : (c + 1) * N_TILE
+                    ].rearrange("b p n -> p b n"),
+                    in_=rotated[:],
+                )
+            waiting.clear()
+
         def project_and_rotate(t, c, w):
             columns = slice(c * N_TILE, (c + 1) * N_TILE)
             pairs = slice(c * CHUNK_PAIRS, (c + 1) * CHUNK_PAIRS)
-            product = products.tile([P, 2, BATCH, CHUNK_PAIRS, 2], F32)
+            product = products.tile([P, BATCH, 2, CHUNK_PAIRS, 2], F32)
+            first = (t, c, w) == (0, 0, 0)
+            last = (t, c, w) == (POS_TILES - 1, CHUNKS - 1, 1)
             for b in range(BATCH):
-                acc = psum_acc.tile([P, N_TILE], F32)
+                acc = psum_acc.tile([P, N_TILE], F32, name="acc")
                 for g in range(PASSES):
                     plane_start = 4 * (PASSES * w + g)
                     nc.tensor.matmul_mx(
@@ -266,8 +292,10 @@ def tile_ropemaskedattentionhead_pa_kernel(
                         start=(g == 0),
                         stop=(g == PASSES - 1),
                     )
+                if last and b == BATCH - 1:
+                    add_on_tensor_engine()
                 nc.vector.tensor_tensor(
-                    out=product[:, :, b, :, :],
+                    out=product[:, b],
                     in0=acc[:]
                     .rearrange("p (i h) -> p h i", h=2)
                     .unsqueeze(3)
@@ -275,10 +303,21 @@ def tile_ropemaskedattentionhead_pa_kernel(
                     in1=table[:, t, :, pairs, :],
                     op=ALU.mult,
                 )
-            if (t, c, w) == (POS_TILES - 1, CHUNKS - 1, 1):
-                for b in range(BATCH):
-                    add_and_store(nc.vector, product, t, c, w, b, 1)
-            else:
+                if first:
+                    add_and_store(nc.gpsimd, product, t, c, w, b, 1)
+                for late in late_adds:
+                    add_and_store(nc.vector, late[0], late[1], late[2], late[3], late[4], 1)
+                late_adds.clear()
+            if last:
+                add_and_store(nc.gpsimd, product, t, c, w, 0, 1)
+                add_and_store(nc.vector, product, t, c, w, 1, 1)
+            elif (t, c, w) == (POS_TILES - 1, 0, 1):
+                add_and_store(nc.gpsimd, product, t, c, w, 0, 1)
+                waiting.append((product, t, c, w, 1))
+            elif (t, c, w) == (POS_TILES - 1, CHUNKS - 1, 0):
+                add_and_store(nc.gpsimd, product, t, c, w, 0, 1)
+                late_adds.append((product, t, c, w, 1))
+            elif not first:
                 add_and_store(nc.gpsimd, product, t, c, w, 0, BATCH)
 
         for c in range(CHUNKS):
@@ -291,7 +330,7 @@ def tile_ropemaskedattentionhead_pa_kernel(
             finish_table(0, c * CHUNK_PAIRS, CHUNK_PAIRS)
         for t in range(1, POS_TILES):
             start_table(t, 0, PAIRS, FINE_STEP)
-        for t in range(1, POS_TILES - 1):
+        for t in range(1, POS_TILES):
             reduce_angle(t, 0)
         for b in range(BATCH):
             flip_x(b, 0)
@@ -305,8 +344,6 @@ def tile_ropemaskedattentionhead_pa_kernel(
                     flip_x(b, t + 1)
             project_and_rotate(t, 0, 1)
             if more:
-                if t == 0:
-                    reduce_angle(POS_TILES - 1, 0)
                 finish_table(t + 1, 0, PAIRS)
                 quantise_x(t + 1, 0, BATCH)
             project_and_rotate(t, 1, 0)

import math
from contextlib import ExitStack

import concourse.mybir as mybir
from concourse.masks import make_identity

F32 = mybir.dt.float32
BF16 = mybir.dt.bfloat16
I32 = mybir.dt.int32
U32 = mybir.dt.uint32
U8 = mybir.dt.uint8
FP8X4 = mybir.dt.float8_e4m3fn_x4
ALU = mybir.AluOpType
ACT = mybir.ActivationFunctionType

P = 128
BATCH = 2
POSITIONS = 512
D_IN = 1024
D_OUT = 1024
PAIRS = D_OUT // 2
POS_TILES = POSITIONS // P
K_PASS = 4 * P
PASSES = D_IN // K_PASS
N_TILE = 512
CHUNKS = D_OUT // N_TILE
CHUNK_PAIRS = N_TILE // 2
WORDS_PER_PASS = K_PASS // 2
FINE = 16
COARSE = PAIRS // FINE

FINE_STEP = 32

RATIO = 10000.0 ** (-2.0 / D_OUT)

FLOPS = 2 * BATCH * POSITIONS * D_IN * 2 * D_OUT


def tile_ropemaskedattentionhead_pa_kernel(
    tc, x, w_q_words, w_q_scales, w_k_words, w_k_scales, out_0, out_1
):
    nc = tc.nc
    weights = ((w_q_words, w_q_scales, out_0), (w_k_words, w_k_scales, out_1))

    with ExitStack() as ctx:
        keep = ctx.enter_context(tc.tile_pool(name="keep", bufs=1))
        stage = ctx.enter_context(tc.tile_pool(name="stage", bufs=2))
        products = ctx.enter_context(tc.tile_pool(name="products", bufs=4))
        results = ctx.enter_context(tc.tile_pool(name="results", bufs=8))
        psum_x = ctx.enter_context(tc.psum_pool(name="psum_x", bufs=2))
        psum_acc = ctx.enter_context(tc.psum_pool(name="psum_acc", bufs=6))
        ctx.enter_context(tc.manual_schedule())

        x_sb = keep.tile([P, BATCH, POS_TILES, D_IN], BF16)
        x_codes = keep.tile([P, POS_TILES, BATCH, PASSES * P], U32, align_bytes=64)
        x_scales = keep.tile([P, POS_TILES, BATCH, PASSES * P], U8, align_bytes=64)
        w_codes = keep.tile([P, 2, PASSES, D_OUT], U32, align_bytes=64)
        w_planes = keep.tile([P, D_OUT], U8, align_bytes=64)
        identity = keep.tile([P, P], F32)
        fine = keep.tile([P, FINE], F32)
        coarse = keep.tile([P, COARSE], F32)
        table_warmer = keep.tile([P, 1], F32)
        theta = keep.tile([P, PAIRS], F32)
        position = keep.tile([P, POS_TILES], I32)
        turns = keep.tile([P, POS_TILES], F32)
        table = keep.tile([P, POS_TILES, 2, PAIRS, 2], F32)
        all_phases = keep.tile([P, POS_TILES, 3, PAIRS], F32)
        early_whole = keep.tile([P, POS_TILES, PAIRS], I32)

        def load_x(b, t):
            nc.sync.dma_start(out=x_sb[:, b, t, :], in_=x[b, t * P : (t + 1) * P, :])

        def load_weight_scales(w):
            scales = weights[w][1]
            for quadrant in range(4):
                first = 32 * quadrant + 4 * PASSES * w
                nc.sync.dma_start(
                    out=w_planes[first : first + 4 * PASSES, :].bitcast(I32),
                    in_=scales[:, 4 * quadrant : 4 * quadrant + 4, :].bitcast(I32),
                )

        def load_weight_codes(w, c):
            columns = slice(c * N_TILE, (c + 1) * N_TILE)
            for g in range(PASSES):
                words = weights[w][0][g].rearrange("p n v -> p (n v)").bitcast(I32)
                nc.sync.dma_start(out=w_codes[:, w, g, columns].bitcast(I32), in_=words[:, columns])

        nc.vector.memset(fine[:, 0:1], 1.0)
        nc.scalar.activation(out=table_warmer[:], in_=fine[:, 0:1], func=ACT.Sin)

        nc.vector.memset(w_planes[:].bitcast(I32), 0)
        for b in range(BATCH):
            load_x(b, 0)
        for w in range(2):
            load_weight_scales(w)
            load_weight_codes(w, 0)
        for b in range(BATCH):
            load_x(b, 1)
        for w in range(2):
            load_weight_codes(w, 1)
        for t in range(2, POS_TILES):
            for b in range(BATCH):
                load_x(b, t)

        nc.gpsimd.iota(position[:], pattern=[[P, POS_TILES]], base=0, channel_multiplier=1)
        make_identity(nc, identity[:])

        nc.vector.memset(coarse[:, 0:1], 1.0)
        n = 1
        while n < COARSE:
            if n < FINE:
                nc.vector.tensor_scalar_mul(
                    out=fine[:, n : 2 * n], in0=fine[:, 0:n], scalar1=RATIO**n
                )
            nc.vector.tensor_scalar_mul(
                out=coarse[:, n : 2 * n], in0=coarse[:, 0:n], scalar1=RATIO ** (FINE * n)
            )
            n = 2 * n
        nc.vector.tensor_scalar_mul(
            out=turns[:], in0=position[:], scalar1=1.0 / (2.0 * math.pi * RATIO)
        )

        def build_theta(c):
            rows = CHUNK_PAIRS // FINE
            nc.vector.tensor_tensor(
                out=theta[:, c * CHUNK_PAIRS : (c + 1) * CHUNK_PAIRS].rearrange(
                    "p (a b) -> p a b", b=FINE
                ),
                in0=coarse[:, c * rows : (c + 1) * rows].unsqueeze(2).to_broadcast([P, rows, FINE]),
                in1=fine[:].unsqueeze(1).to_broadcast([P, rows, FINE]),
                op=ALU.mult,
            )

        def reduced_pairs(t, step):
            last_position = P * (t + 1) - 1
            n = 0
            while n < PAIRS and last_position * RATIO ** (n - 1) > 0.49 * 2.0 * math.pi:
                n += step
            return n

        whole_turns = {}
        phases = {}

        def start_table(t, first_pair, count, step):
            n = min(max(reduced_pairs(t, step) - first_pair, 0), count)
            phase = all_phases[:, t, :, first_pair : first_pair + count]
            phases[(t, first_pair)] = (phase, n)
            if n > 0 and t == 0:
                whole = stage.tile([P, n], U32, name="whole")
                nc.scalar.activation(
                    out=whole[:],
                    in_=theta[:, first_pair : first_pair + n],
                    func=ACT.Copy,
                    scale=turns[:, t : t + 1],
                )
                whole_turns[(t, first_pair)] = whole[:].bitcast(I32)
            if n < count:
                nc.scalar.activation(
                    out=phase[:, 0, n:count],
                    in_=theta[:, first_pair + n : first_pair + count],
                    func=ACT.Copy,
                    scale=turns[:, t : t + 1],
                )

        def whole_turns_early(t):
            n = reduced_pairs(t, FINE_STEP)
            nc.gpsimd.tensor_scalar(
                out=early_whole[:, t, 0:n],
                in0=theta[:, 0:n],
                scalar1=turns[:, t : t + 1],
                scalar2=0.0,
                op0=ALU.mult,
                op1=ALU.add,
            )
            whole_turns[(t, 0)] = early_whole[:, t, 0:n]

        def reduce_angle(t, first_pair):
            phase, n = phases[(t, first_pair)]
            if n > 0:
                nc.vector.scalar_tensor_tensor(
                    out=phase[:, 0, 0:n],
                    in0=theta[:, first_pair : first_pair + n],
                    scalar=turns[:, t : t + 1],
                    in1=whole_turns[(t, first_pair)],
                    op0=ALU.mult,
                    op1=ALU.subtract,
                )

        def finish_table(t, first_pair, count):
            pairs = slice(first_pair, first_pair + count)
            phase, n = phases[(t, first_pair)]
            nc.scalar.activation(out=phase[:, 1, :], in_=phase[:, 0, :], func=ACT.Abs)
            nc.scalar.activation(
                out=phase[:, 1, :], in_=phase[:, 1, :], func=ACT.Copy, scale=-1.0, bias=0.25
            )
            nc.scalar.mul(out=phase[:, 2, :], in_=phase[:, 0, :], mul=-1.0)
            for half in range(2):
                first = 1 - half
                nc.scalar.activation(
                    out=table[:, t, half, pairs, :],
                    in_=phase[:, first : first + 2, :].rearrange("p w i -> p i w"),
                    func=ACT.Sin,
                    scale=2.0 * math.pi,
                )

        grouped_x = {}

        def flip_x(b, t):
            x_words = x_sb[:, b, t, :].bitcast(F32)
            flipped = psum_x.tile([P, PASSES, 2, P], F32)
            for g in range(PASSES):
                for u in range(2):
                    nc.tensor.transpose(
                        flipped[:, g, u, :],
                        x_words[:, WORDS_PER_PASS * g + u : WORDS_PER_PASS * (g + 1) : 2],
                        identity[:],
                    )
            if b == 0:
                both_batches = stage.tile([P, BATCH, PASSES, P, 4], BF16, align_bytes=64, name="grouped")
                grouped_x[t] = both_batches
            grouped = grouped_x[t][:, b].rearrange("p g r v -> p g (r v)").bitcast(F32)
            copier = nc.vector.tensor_copy if t == 0 else nc.scalar.copy
            copier(
                out=grouped.rearrange("p g (r u) -> p g r u", u=2),
                in_=flipped[:].rearrange("p g u r -> p g r u"),
            )

        def quantise_x(t, first_batch, batches):
            chosen = slice(first_batch, first_batch + batches)
            nc.vector.quantize_mx(
                out=x_codes[:, t, chosen, :].rearrange("p b n -> p (b n)").bitcast(FP8X4),
                scales=x_scales[:, t, chosen, :].rearrange("p b n -> p (b n)"),
                in_=grouped_x[t][:, chosen].rearrange("p b g r v -> p (b g r v)"),
            )

        def add_and_store(adder, product, t, c, w, first_batch, batches):
            chosen = slice(first_batch, first_batch + batches)
            rotated = results.tile([P, batches, N_TILE], F32)
            adder.tensor_tensor(
                out=rotated[:],
                in0=product[:, chosen, 0].rearrange("p b i w -> p b (i w)"),
                in1=product[:, chosen, 1].rearrange("p b i w -> p b (i w)"),
                op=ALU.add,
            )
            nc.sync.dma_start(
                out=weights[w][2][
                    chosen, t * P : (t + 1) * P, c * N_TILE : (c + 1) * N_TILE
                ].rearrange("b p n -> p b n"),
                in_=rotated[:],
            )

        late_adds = []
        waiting = []

        def add_on_tensor_engine():
            for product, t, c, w, b in waiting:
                total = psum_acc.tile([P, N_TILE], F32, name="acc")
                for h in range(2):
                    nc.tensor.matmul(
                        out=total[:],
                        lhsT=identity[:],
                        rhs=product[:, b, h].rearrange("p i v -> p (i v)"),
                        start=(h == 0),
                        stop=(h == 1),
                    )
                rotated = results.tile([P, 1, N_TILE], F32, name="rotated")
                nc.scalar.copy(out=rotated[:, 0, :], in_=total[:])
                nc.sync.dma_start(
                    out=weights[w][2][
                        b : b + 1, t * P : (t + 1) * P, c * N_TILE : (c + 1) * N_TILE
                    ].rearrange("b p n -> p b n"),
                    in_=rotated[:],
                )
            waiting.clear()

        def project_and_rotate(t, c, w):
            columns = slice(c * N_TILE, (c + 1) * N_TILE)
            pairs = slice(c * CHUNK_PAIRS, (c + 1) * CHUNK_PAIRS)
            product = products.tile([P, BATCH, 2, CHUNK_PAIRS, 2], F32)
            first = (t, c, w) == (0, 0, 0)
            last = (t, c, w) == (POS_TILES - 1, CHUNKS - 1, 1)
            for b in range(BATCH):
                acc = psum_acc.tile([P, N_TILE], F32, name="acc")
                for g in range(PASSES):
                    plane_start = 4 * (PASSES * w + g)
                    nc.tensor.matmul_mx(
                        out=acc[:],
                        lhsT=x_codes[:, t, b, g * P : (g + 1) * P].bitcast(FP8X4),
                        lhsT_scale=x_scales[:, t, b, g * P : (g + 1) * P],
                        rhs=w_codes[:, w, g, columns].bitcast(FP8X4),
                        rhs_scale=w_planes[plane_start:P, columns],
                        start=(g == 0),
                        stop=(g == PASSES - 1),
                    )
                if last and b == BATCH - 1:
                    add_on_tensor_engine()
                nc.vector.tensor_tensor(
                    out=product[:, b],
                    in0=acc[:]
                    .rearrange("p (i h) -> p h i", h=2)
                    .unsqueeze(3)
                    .to_broadcast([P, 2, CHUNK_PAIRS, 2]),
                    in1=table[:, t, :, pairs, :],
                    op=ALU.mult,
                )
                if first:
                    add_and_store(nc.gpsimd, product, t, c, w, b, 1)
                for late in late_adds:
                    add_and_store(nc.vector, late[0], late[1], late[2], late[3], late[4], 1)
                late_adds.clear()
            if last:
                add_and_store(nc.gpsimd, product, t, c, w, 0, 1)
                add_and_store(nc.vector, product, t, c, w, 1, 1)
            elif (t, c, w) == (POS_TILES - 1, 0, 1):
                add_and_store(nc.gpsimd, product, t, c, w, 0, 1)
                waiting.append((product, t, c, w, 1))
            elif (t, c, w) == (POS_TILES - 1, CHUNKS - 1, 0):
                add_and_store(nc.gpsimd, product, t, c, w, 0, 1)
                late_adds.append((product, t, c, w, 1))
            elif not first:
                add_and_store(nc.gpsimd, product, t, c, w, 0, BATCH)

        for c in range(CHUNKS):
            build_theta(c)
            start_table(0, c * CHUNK_PAIRS, CHUNK_PAIRS, CHUNK_PAIRS)
        for t in range(1, POS_TILES):
            whole_turns_early(t)
        for c in range(CHUNKS):
            reduce_angle(0, c * CHUNK_PAIRS)
            finish_table(0, c * CHUNK_PAIRS, CHUNK_PAIRS)
        for t in range(1, POS_TILES):
            start_table(t, 0, PAIRS, FINE_STEP)
        for t in range(1, POS_TILES):
            reduce_angle(t, 0)
        for b in range(BATCH):
            flip_x(b, 0)
            quantise_x(0, b, 1)

        for t in range(POS_TILES):
            more = t + 1 < POS_TILES
            project_and_rotate(t, 0, 0)
            if more:
                for b in range(BATCH):
                    flip_x(b, t + 1)
            project_and_rotate(t, 0, 1)
            if more:
                finish_table(t + 1, 0, PAIRS)
                quantise_x(t + 1, 0, BATCH)
            project_and_rotate(t, 1, 0)
            project_and_rotate(t, 1, 1)
